import numpy as np
import ml_dtypes


def mxq(x, axis, fmt="e4m3"):
    dtype, down = {"e4m3": (ml_dtypes.float8_e4m3fn, 7), "e5m2": (ml_dtypes.float8_e5m2, 14)}[fmt]
    v = np.moveaxis(np.asarray(x, np.float32).astype(ml_dtypes.bfloat16).astype(np.float64), axis, -1)
    blocks = v.reshape(v.shape[:-1] + (-1, 32))
    amax = np.abs(blocks).max(-1, keepdims=True)
    byte = np.maximum(np.where(amax > 0, np.frexp(amax)[1] - 1 + 127, 0) - down, 1)
    scale = np.exp2(byte - 127.0)
    codes = (blocks / scale).astype(np.float32).astype(dtype).astype(np.float64)
    return np.moveaxis((codes * scale).reshape(v.shape), -1, axis)


WIDE = False


def mx_kscale(k):
    if not WIDE:
        return np.ones(k)
    levels = np.array([10, -10, 5, -5, 0])
    a = np.random.permutation(np.resize(levels, k // 512 * 4)).reshape(k // 512, 4)
    idx = np.arange(k)
    return np.exp2(a[idx // 512, idx % 128 // 32])


BF16 = ml_dtypes.bfloat16


def bf(x):
    return np.asarray(x, np.float32).astype(BF16)


def f64(x):
    return np.asarray(x).astype(np.float64)


B, C, CK, CV, CO, H, W, P1, P2, P3, P4 = 1, 1024, 256, 256, 1024, 24, 48, 1, 3, 6, 8
PSP_SIZES = (P1, P2, P3, P4)
EPS = 1e-5
N = H * W


def bnrelu(x, gamma, beta, mean, var):
    inv = 1.0 / np.sqrt(var + EPS)
    return np.maximum((x - mean[None, :, None]) * (inv * gamma)[None, :, None] + beta[None, :, None], 0.0)


def psp(x):
    b, c = x.shape[:2]
    outs = []
    for s in PSP_SIZES:
        outs.append(x.reshape(b, c, s, H // s, s, W // s).mean(axis=(3, 5)).reshape(b, c, s * s))
    return np.concatenate(outs, axis=-1)


def setup_inputs():
    s = mx_kscale(C)
    fine = np.random.standard_normal((B, C, H, W))
    coarse = np.random.standard_normal((B, C, P4, P4))
    coarse = np.repeat(np.repeat(coarse, H // P4, axis=2), W // P4, axis=3)
    return {"feats": bf((fine + coarse) * np.sqrt(0.5) * s[None, :, None, None]),
            "Wk": bf(np.random.standard_normal((CK, C)) * 1.5 / np.sqrt(C) / s[None, :]),
            "bk": bf(np.random.standard_normal(CK) * 0.2),
            "gk": bf(1.0 + 0.1 * np.random.standard_normal(CK)),
            "betak": bf(np.random.standard_normal(CK) * 0.2),
            "mk": bf(np.random.standard_normal(CK) * 0.2),
            "vk": bf(np.random.uniform(0.5, 1.5, CK)),
            "Wv": bf(np.random.standard_normal((CV, C)) / np.sqrt(C) / s[None, :]),
            "bv": bf(np.random.standard_normal(CV) * 0.2)}


def reference(feats, Wk, bk, gk, betak, mk, vk, Wv, bv):
    xq = mxq(f64(feats).reshape(B, C, N), 1, "e4m3")
    pre = (mxq(f64(Wk), 1, "e4m3") @ xq) + f64(bk)[None, :, None]
    kf = bnrelu(pre, f64(gk), f64(betak), f64(mk), f64(vk)).reshape(B, CK, H, W)
    keyp = psp(kf)
    val = ((mxq(f64(Wv), 1, "e4m3") @ xq) + f64(bv)[None, :, None]).reshape(B, CV, H, W)
    value = psp(val).transpose(0, 2, 1)
    return kf, keyp, value

@@ -1,0 +1,349 @@
+from contextlib import ExitStack
+
+import concourse.mybir as mybir
+from concourse.masks import make_identity
+
+F32 = mybir.dt.float32
+BF16 = mybir.dt.bfloat16
+I32 = mybir.dt.int32
+U32 = mybir.dt.uint32
+U8 = mybir.dt.uint8
+FP8X4 = mybir.dt.float8_e4m3fn_x4
+ALU = mybir.AluOpType
+ACT = mybir.ActivationFunctionType
+AXIS = mybir.AxisListType
+
+P = 128
+PACK = 4
+K_PASS = P * PACK
+BANK = 512
+
+C = 1024
+PASSES = C // K_PASS
+CK = 256
+CV = 256
+HALVES = CK // P
+H = 24
+W = 48
+N = H * W
+EPS = 1e-5
+
+CHUNK_ROWS = 8
+CHUNK = CHUNK_ROWS * W
+CHUNKS = N // CHUNK
+TILES = CHUNK // P
+ALL_TILES = CHUNKS * TILES
+
+LEVELS = (1, 3, 6, 8)
+FIRST = {1: 0, 3: 1, 6: 10, 8: 46}
+TOKENS = 110
+
+FLOPS = 2 * (CK + CV) * C * N
+
+
+LAG_QUANTISE = 1
+LAG_PROJECT_KEYS = 2
+LAG_LEAVE_KEYS = 3
+LAG_PROJECT_VALUES = 4
+LAG_LEAVE_VALUES = 5
+LAG_POOL_VALUES = 6
+LAG_POOL_KEYS = 6
+POOLED = (8, 6, 3)
+
+
+def tile_apnb_pa_kernel(tc, feats, Wk, bk, gk, betak, mk, vk, Wv, bv, out_0, out_1, out_2):
+    nc = tc.nc
+    with ExitStack() as ctx:
+        keep = ctx.enter_context(tc.tile_pool(name="keep", bufs=1))
+        key_banks = ctx.enter_context(tc.psum_pool(name="key_banks", bufs=2 * HALVES))
+        val_banks = ctx.enter_context(tc.psum_pool(name="val_banks", bufs=3))
+        total = ctx.enter_context(tc.psum_pool(name="total", bufs=1))
+        ctx.enter_context(tc.manual_schedule())
+
+        position = keep.tile([P, ALL_TILES], I32, name="position")
+        nc.gpsimd.iota(position[:], pattern=[[P, ALL_TILES]], base=0, channel_multiplier=1)
+        count = keep.tile([P, 64], F32, name="count")
+        nc.gpsimd.iota(
+            count[:], pattern=[[1, 64]], base=0, channel_multiplier=0, allow_small_or_imprecise_dtypes=True
+        )
+        ident = keep.tile([P, P], F32, name="ident")
+        make_identity(nc, ident[:])
+        cell_size = keep.tile([P, P], F32, name="cell_size")
+        nc.gpsimd.memset(cell_size[:, TOKENS:P], 1.0)
+        for s in LEVELS:
+            nc.gpsimd.memset(cell_size[:, FIRST[s] : FIRST[s] + s * s], float(N // (s * s)))
+
+        params_bf = keep.tile([P, CK], BF16, name="params_bf")
+        nc.vector.memset(params_bf[:], 0.0)
+        for row, values in enumerate((bv, bk, gk, betak, mk, vk)):
+            nc.scalar.dma_start(out=params_bf[row : row + 1, :], in_=values.rearrange("(o c) -> o c", o=1))
+
+        def load_weight(w, name):
+            rows = keep.tile([P, HALVES, C], BF16, name=name)
+            nc.sync.dma_start(out=rows[:], in_=w.rearrange("(r p) k -> p r k", p=P))
+            return rows
+
+        wk_rows = load_weight(Wk, "wk_rows")
+
+        x_rows = feats.rearrange("b (s q e) h w -> e q (b s) (h w)", s=2 * PASSES, e=2)
+        raw = [keep.tile([P, PASSES, PACK, CHUNK], BF16, name="raw%d" % c) for c in range(CHUNKS)]
+
+        def load_chunk(c):
+            split = raw[c][:].rearrange("p g (u e) n -> p (g u) e n", e=2)
+            for e in range(2):
+                nc.sync.dma_start(out=split[:, :, e, :], in_=x_rows[e][:, :, c * CHUNK : (c + 1) * CHUNK])
+
+        load_chunk(0)
+        wv_rows = load_weight(Wv, "wv_rows")
+        load_chunk(1)
+        load_chunk(2)
+
+        one = keep.tile([P, 1], F32, name="one")
+        nc.vector.memset(one[:], 1.0)
+        nc.scalar.activation(out=one[:], in_=one[:], func=ACT.Sqrt)
+
+        shifted = keep.tile([P, 2, ALL_TILES], I32, name="shifted")
+        product = keep.tile([P, 2, ALL_TILES], I32, name="product")
+
+        def third(out, in_, also_shift_left):
+            like = product[:, 0 : in_.shape[1], :]
+            nc.vector.tensor_scalar(out=like, in0=in_, scalar1=683.0, scalar2=None, op0=ALU.mult)
+            nc.vector.tensor_scalar(
+                out=out,
+                in0=like,
+                scalar1=11,
+                scalar2=also_shift_left,
+                op0=ALU.logical_shift_right,
+                op1=ALU.logical_shift_left,
+            )
+
+        place = keep.tile([P, 2, ALL_TILES], I32, name="place")
+        nc.vector.tensor_scalar(
+            out=shifted[:, 0:1, :], in0=position[:].unsqueeze(1), scalar1=4, scalar2=None, op0=ALU.logical_shift_right
+        )
+        third(place[:, 0:1, :], shifted[:, 0:1, :], 1)
+        nc.vector.scalar_tensor_tensor(
+            out=place[:, 1, :], in0=place[:, 0, :], scalar=-24.0, in1=position[:], op0=ALU.mult, op1=ALU.add
+        )
+        band_cell = keep.tile([P, 3, 2, ALL_TILES], I32, name="band_cell")
+        nc.vector.tensor_scalar(out=band_cell[:, 0], in0=place[:], scalar1=4, scalar2=None, op0=ALU.logical_shift_right)
+        nc.vector.tensor_scalar(out=band_cell[:, 1], in0=place[:], scalar1=3, scalar2=None, op0=ALU.logical_shift_right)
+        nc.vector.tensor_scalar(out=shifted[:], in0=place[:], scalar1=1, scalar2=None, op0=ALU.logical_shift_right)
+        third(band_cell[:, 2], shifted[:], 0)
+        cell = keep.tile([P, 3, ALL_TILES], F32, name="cell")
+        pool = keep.tile([P, ALL_TILES, P], F32, name="pool")
+        nc.vector.memset(pool[:, :, 0:1], 1.0)
+        nc.vector.memset(pool[:, :, TOKENS:P], 0.0)
+        for l, s in enumerate(LEVELS[1:]):
+            nc.vector.scalar_tensor_tensor(
+                out=cell[:, l, :],
+                in0=band_cell[:, l, 0, :],
+                scalar=float(s),
+                in1=band_cell[:, l, 1, :],
+                op0=ALU.mult,
+                op1=ALU.add,
+            )
+            shape = [P, ALL_TILES, s * s]
+            nc.vector.tensor_tensor(
+                out=pool[:, :, FIRST[s] : FIRST[s] + s * s],
+                in0=count[:, 0 : s * s].unsqueeze(1).to_broadcast(shape),
+                in1=cell[:, l, :].unsqueeze(2).to_broadcast(shape),
+                op=ALU.is_equal,
+            )
+        weight = keep.tile([P, P], F32, name="weight")
+        nc.vector.reciprocal(out=weight[:], in_=cell_size[:])
+        nc.vector.tensor_tensor(
+            out=pool[:], in0=pool[:], in1=weight[:].unsqueeze(1).to_broadcast([P, ALL_TILES, P]), op=ALU.mult
+        )
+
+        def quantise_weight(rows, name, psum, tag):
+            w_grouped = keep.tile([P, PASSES, HALVES * P, PACK], BF16, name=name + "_grouped", align_bytes=64)
+            w_pairs = w_grouped[:].bitcast(F32)
+            for r, copy in enumerate((nc.vector.tensor_copy, nc.scalar.copy)):
+                words = rows[:, r, :].bitcast(F32)
+                bank = psum.tile([P, BANK], F32, name=name + "_bank", tag=tag)
+                for s in range(BANK // P):
+                    nc.tensor.transpose(bank[:, s * P : (s + 1) * P], words[:, s * P : (s + 1) * P], ident[:])
+                copy(
+                    out=w_pairs[:, :, r * P : (r + 1) * P, :],
+                    in_=bank[:].rearrange("p (g u o) -> p g o u", g=PASSES, u=2),
+                )
+            codes = keep.tile([P, PASSES, HALVES * P], U32, name=name + "_codes", align_bytes=64)
+            scales = keep.tile([P, PASSES, HALVES * P], U8, name=name + "_scales", align_bytes=64)
+            nc.vector.quantize_mx(
+                out=codes[:].rearrange("p g o -> p (g o)").bitcast(FP8X4),
+                scales=scales[:].rearrange("p g o -> p (g o)"),
+                in_=w_grouped[:].rearrange("p g o t -> p (g o t)"),
+            )
+            return codes, scales
+
+        params = keep.tile([P, CK], F32, name="params")
+        nc.vector.tensor_copy(out=params[:], in_=params_bf[:])
+        wk_codes, wk_scales = quantise_weight(wk_rows, "wk", key_banks, "keys")
+
+        params_bank = val_banks.tile([P, BANK], F32, name="params_bank", tag="vals")
+        flipped_params = params_bank[:, 0 : HALVES * P].rearrange("p (m r) -> p m r", m=HALVES)
+        for m in range(HALVES):
+            nc.tensor.transpose(flipped_params[:, m, :], params[:, m * P : (m + 1) * P], ident[:])
+        by_channel = keep.tile([P, HALVES, 6], F32, name="by_channel")
+        nc.vector.tensor_copy(out=by_channel[:], in_=flipped_params[:, :, 0:6])
+        spread = keep.tile([P, HALVES], F32, name="spread")
+        std = keep.tile([P, HALVES], F32, name="std")
+        scale = keep.tile([P, HALVES], F32, name="scale")
+        shift = keep.tile([P, HALVES], F32, name="shift")
+        nc.vector.tensor_scalar_add(out=spread[:], in0=by_channel[:, :, 5], scalar1=EPS)
+        nc.scalar.activation(out=std[:], in_=spread[:], func=ACT.Sqrt)
+
+        value_sum = total.tile([P, BANK], F32, name="value_sum")
+        nc.tensor.matmul(
+            out=value_sum[:, 0:CV], lhsT=ident[:, 0:1].to_broadcast([P, P]), rhs=params[:], start=True, stop=False
+        )
+
+        nc.vector.reciprocal(out=scale[:], in_=std[:])
+        nc.vector.tensor_mul(out=scale[:], in0=scale[:], in1=by_channel[:, :, 2])
+        nc.vector.tensor_sub(out=shift[:], in0=by_channel[:, :, 1], in1=by_channel[:, :, 4])
+        nc.vector.tensor_mul(out=shift[:], in0=shift[:], in1=scale[:])
+        nc.vector.tensor_add(out=shift[:], in0=shift[:], in1=by_channel[:, :, 3])
+
+        grouped = keep.tile([P, ALL_TILES, PASSES, P, PACK], BF16, name="grouped", align_bytes=64)
+        x_codes = keep.tile([P, ALL_TILES, PASSES, P], U32, name="x_codes", align_bytes=64)
+        x_scales = keep.tile([P, ALL_TILES, PASSES, P], U8, name="x_scales", align_bytes=64)
+        kf = keep.tile([P, HALVES, N], F32, name="kf")
+        kf_out = out_0.rearrange("b (m p) h w -> p (b m) (h w)", p=P)
+        sums = keep.tile([P, HALVES, TOKENS], F32, name="sums")
+        val_t = keep.tile([P, ALL_TILES, CV], F32, name="val_t")
+        key_bank = {}
+        val_bank = {}
+
+        def regroup(i):
+            c, j = divmod(i, TILES)
+            for g, copy in enumerate((nc.vector.tensor_copy, nc.scalar.copy)):
+                copy(
+                    out=grouped[:, i, g].rearrange("p (n r) t -> p n t r", r=4),
+                    in_=raw[c][:, g, :, j * P : (j + 1) * P].rearrange("p t (n r) -> p n t r", r=4),
+                )
+
+        def quantise(i):
+            nc.vector.quantize_mx(
+                out=x_codes[:, i].rearrange("p g n -> p (g n)").bitcast(FP8X4),
+                scales=x_scales[:, i].rearrange("p g n -> p (g n)"),
+                in_=grouped[:, i].rearrange("p g n t -> p (g n t)"),
+            )
+
+        def project_keys(i):
+            c, j = divmod(i, TILES)
+            for m in range(HALVES):
+                if j == 0:
+                    key_bank[c, m] = key_banks.tile([P, BANK], F32, name="key_bank", tag="keys")
+                for g in range(PASSES):
+                    nc.tensor.matmul_mx(
+                        out=key_bank[c, m][:, j * P : (j + 1) * P],
+                        lhsT=wk_codes[:, g, m * P : (m + 1) * P].bitcast(FP8X4),
+                        lhsT_scale=wk_scales[:, g, m * P : (m + 1) * P],
+                        rhs=x_codes[:, i, g, :].bitcast(FP8X4),
+                        rhs_scale=x_scales[:, i, g, :],
+                        start=(g == 0),
+                        stop=(g == PASSES - 1),
+                    )
+
+        def project_values(i):
+            val_bank[i] = val_banks.tile([P, BANK], F32, name="val_bank", tag="vals")
+            for g in range(PASSES):
+                nc.tensor.matmul_mx(
+                    out=val_bank[i][:, 0:CV],
+                    lhsT=x_codes[:, i, g, :].bitcast(FP8X4),
+                    lhsT_scale=x_scales[:, i, g, :],
+                    rhs=wv_codes[:, g, :].bitcast(FP8X4),
+                    rhs_scale=wv_scales[:, g, :],
+                    start=(g == 0),
+                    stop=(g == PASSES - 1),
+                )
+
+        def leave_values(i):
+            nc.scalar.copy(out=val_t[:, i, :], in_=val_bank[i][:, 0:CV])
+
+        def leave_keys(i):
+            c, j = divmod(i, TILES)
+            if j == TILES - 1:
+                cols = slice(c * CHUNK, (c + 1) * CHUNK)
+                for m in range(HALVES):
+                    nc.scalar.activation(
+                        out=kf[:, m, cols],
+                        in_=key_bank[c, m][:, 0:CHUNK],
+                        func=ACT.Relu,
+                        bias=shift[:, m : m + 1],
+                        scale=scale[:, m : m + 1],
+                    )
+                nc.sync.dma_start(out=kf_out[:, :, cols], in_=kf[:, :, cols])
+
+        def pool_values(i):
+            nc.tensor.matmul(
+                out=value_sum[:, 0:CV], lhsT=pool[:, i, :], rhs=val_t[:, i, :], start=False, stop=(i == ALL_TILES - 1)
+            )
+
+        def pool_keys(i):
+            c, j = divmod(i, TILES)
+            s = POOLED[j]
+            if s == 3:
+                nc.vector.tensor_reduce(
+                    out=sums[:, :, FIRST[3] + 3 * c : FIRST[3] + 3 * (c + 1)],
+                    in_=sums[:, :, FIRST[6] + 12 * c : FIRST[6] + 12 * (c + 1)].rearrange(
+                        "p m (b c x) -> p m c b x", b=2, x=2
+                    ),
+                    axis=AXIS.XY,
+                    op=ALU.add,
+                )
+                return
+            rows = H // s
+            first = c * CHUNK_ROWS // rows
+            after = (c + 1) * CHUNK_ROWS // rows
+            for m in range(HALVES):
+                nc.vector.tensor_reduce(
+                    out=sums[:, m, FIRST[s] + first * s : FIRST[s] + after * s].rearrange("p (b c) -> p b c", c=s),
+                    in_=kf[:, m, first * rows * W : after * rows * W].rearrange(
+                        "p (b r c x) -> p b c r x", r=rows, c=s, x=W // s
+                    ),
+                    axis=AXIS.XY,
+                    op=ALU.add,
+                )
+
+        def due(turn, lag):
+            return 0 <= turn - lag < ALL_TILES
+
+        def take_turn(turn):
+            if due(turn, 0):
+                regroup(turn)
+            if due(turn, LAG_QUANTISE):
+                quantise(turn - LAG_QUANTISE)
+            if due(turn, LAG_PROJECT_KEYS):
+                project_keys(turn - LAG_PROJECT_KEYS)
+            if due(turn, LAG_LEAVE_KEYS):
+                leave_keys(turn - LAG_LEAVE_KEYS)
+            if due(turn, LAG_PROJECT_VALUES):
+                project_values(turn - LAG_PROJECT_VALUES)
+            if due(turn, LAG_LEAVE_VALUES):
+                leave_values(turn - LAG_LEAVE_VALUES)
+            if due(turn, LAG_POOL_VALUES):
+                pool_values(turn - LAG_POOL_VALUES)
+            if due(turn, LAG_POOL_KEYS):
+                pool_keys(turn - LAG_POOL_KEYS)
+
+        for turn in range(TILES):
+            take_turn(turn)
+        wv_codes, wv_scales = quantise_weight(wv_rows, "wv", val_banks, "vals")
+        for turn in range(TILES, ALL_TILES + LAG_POOL_KEYS):
+            take_turn(turn)
+
+        value = keep.tile([P, CV], F32, name="value")
+        nc.scalar.copy(out=value[:], in_=value_sum[:, 0:CV])
+        nc.sync.dma_start(out=out_2.rearrange("b t c -> (b t) c"), in_=value[0:TOKENS, :])
+
+        nc.vector.tensor_reduce(out=sums[:, :, 0:1], in_=sums[:, :, FIRST[3] : FIRST[6]], axis=AXIS.X, op=ALU.add)
+        keyp = keep.tile([P, HALVES, TOKENS], F32, name="keyp")
+        nc.vector.tensor_tensor(
+            out=keyp[:],
+            in0=sums[:],
+            in1=weight[:, 0:TOKENS].unsqueeze(1).to_broadcast([P, HALVES, TOKENS]),
+            op=ALU.mult,
+        )
+        nc.sync.dma_start(out=out_1.rearrange("b (m p) t -> p (b m) t", p=P), in_=keyp[:])

@@ -42,12 +42,11 @@ FLOPS = 2 * (CK + CV) * C * N
 
 
 LAG_QUANTISE = 1
-LAG_PROJECT_KEYS = 2
-LAG_LEAVE_KEYS = 3
-LAG_PROJECT_VALUES = 4
-LAG_LEAVE_VALUES = 5
-LAG_POOL_VALUES = 6
-LAG_POOL_KEYS = 6
+LAG_PROJECT = 3
+LAG_LEAVE = 5
+LAG_POOL_VALUES = 7
+LAG_POOL_KEYS = 8
+LAST_TURN = ALL_TILES + LAG_POOL_KEYS
 POOLED = (8, 6, 3)
 
 
@@ -97,10 +96,6 @@ def tile_apnb_pa_kernel(tc, feats, Wk, bk, gk, betak, mk, vk, Wv, bv, out_0, out
         wv_rows = load_weight(Wv, "wv_rows")
         load_chunk(1)
         load_chunk(2)
-
-        one = keep.tile([P, 1], F32, name="one")
-        nc.vector.memset(one[:], 1.0)
-        nc.scalar.activation(out=one[:], in_=one[:], func=ACT.Sqrt)
 
         shifted = keep.tile([P, 2, ALL_TILES], I32, name="shifted")
         product = keep.tile([P, 2, ALL_TILES], I32, name="product")
@@ -156,18 +151,21 @@ def tile_apnb_pa_kernel(tc, feats, Wk, bk, gk, betak, mk, vk, Wv, bv, out_0, out
             out=pool[:], in0=pool[:], in1=weight[:].unsqueeze(1).to_broadcast([P, ALL_TILES, P]), op=ALU.mult
         )
 
-        def quantise_weight(rows, name, psum, tag):
+        def flip_weight(rows, name, psum, tag):
             w_grouped = keep.tile([P, PASSES, HALVES * P, PACK], BF16, name=name + "_grouped", align_bytes=64)
             w_pairs = w_grouped[:].bitcast(F32)
-            for r, copy in enumerate((nc.vector.tensor_copy, nc.scalar.copy)):
+            for r in range(HALVES):
                 words = rows[:, r, :].bitcast(F32)
                 bank = psum.tile([P, BANK], F32, name=name + "_bank", tag=tag)
                 for s in range(BANK // P):
                     nc.tensor.transpose(bank[:, s * P : (s + 1) * P], words[:, s * P : (s + 1) * P], ident[:])
-                copy(
+                nc.scalar.copy(
                     out=w_pairs[:, :, r * P : (r + 1) * P, :],
                     in_=bank[:].rearrange("p (g u o) -> p g o u", g=PASSES, u=2),
                 )
+            return w_grouped
+
+        def quantise_weight(w_grouped, name):
             codes = keep.tile([P, PASSES, HALVES * P], U32, name=name + "_codes", align_bytes=64)
             scales = keep.tile([P, PASSES, HALVES * P], U8, name=name + "_scales", align_bytes=64)
             nc.vector.quantize_mx(
@@ -179,31 +177,31 @@ def tile_apnb_pa_kernel(tc, feats, Wk, bk, gk, betak, mk, vk, Wv, bv, out_0, out
 
         params = keep.tile([P, CK], F32, name="params")
         nc.vector.tensor_copy(out=params[:], in_=params_bf[:])
-        wk_codes, wk_scales = quantise_weight(wk_rows, "wk", key_banks, "keys")
+        wk_grouped = flip_weight(wk_rows, "wk", key_banks, "keys")
 
         params_bank = val_banks.tile([P, BANK], F32, name="params_bank", tag="vals")
         flipped_params = params_bank[:, 0 : HALVES * P].rearrange("p (m r) -> p m r", m=HALVES)
         for m in range(HALVES):
             nc.tensor.transpose(flipped_params[:, m, :], params[:, m * P : (m + 1) * P], ident[:])
         by_channel = keep.tile([P, HALVES, 6], F32, name="by_channel")
-        nc.vector.tensor_copy(out=by_channel[:], in_=flipped_params[:, :, 0:6])
-        spread = keep.tile([P, HALVES], F32, name="spread")
-        std = keep.tile([P, HALVES], F32, name="std")
+        minus_half = keep.tile([P, HALVES], F32, name="minus_half")
+        nc.gpsimd.memset(minus_half[:], -0.5)
         scale = keep.tile([P, HALVES], F32, name="scale")
         shift = keep.tile([P, HALVES], F32, name="shift")
-        nc.vector.tensor_scalar_add(out=spread[:], in0=by_channel[:, :, 5], scalar1=EPS)
-        nc.scalar.activation(out=std[:], in_=spread[:], func=ACT.Sqrt)
+
+        def fold_norm():
+            nc.scalar.copy(out=by_channel[:], in_=flipped_params[:, :, 0:6])
+            nc.gpsimd.tensor_scalar_add(out=scale[:], in0=by_channel[:, :, 5], scalar1=EPS)
+            nc.gpsimd.tensor_tensor(out=scale[:], in0=scale[:], in1=minus_half[:], op=ALU.pow)
+            nc.gpsimd.tensor_mul(out=scale[:], in0=scale[:], in1=by_channel[:, :, 2])
+            nc.gpsimd.tensor_sub(out=shift[:], in0=by_channel[:, :, 1], in1=by_channel[:, :, 4])
+            nc.gpsimd.tensor_mul(out=shift[:], in0=shift[:], in1=scale[:])
+            nc.gpsimd.tensor_add(out=shift[:], in0=shift[:], in1=by_channel[:, :, 3])
 
         value_sum = total.tile([P, BANK], F32, name="value_sum")
         nc.tensor.matmul(
             out=value_sum[:, 0:CV], lhsT=ident[:, 0:1].to_broadcast([P, P]), rhs=params[:], start=True, stop=False
         )
-
-        nc.vector.reciprocal(out=scale[:], in_=std[:])
-        nc.vector.tensor_mul(out=scale[:], in0=scale[:], in1=by_channel[:, :, 2])
-        nc.vector.tensor_sub(out=shift[:], in0=by_channel[:, :, 1], in1=by_channel[:, :, 4])
-        nc.vector.tensor_mul(out=shift[:], in0=shift[:], in1=scale[:])
-        nc.vector.tensor_add(out=shift[:], in0=shift[:], in1=by_channel[:, :, 3])
 
         grouped = keep.tile([P, ALL_TILES, PASSES, P, PACK], BF16, name="grouped", align_bytes=64)
         x_codes = keep.tile([P, ALL_TILES, PASSES, P], U32, name="x_codes", align_bytes=64)
@@ -311,27 +309,28 @@ def tile_apnb_pa_kernel(tc, feats, Wk, bk, gk, betak, mk, vk, Wv, bv, out_0, out
             return 0 <= turn - lag < ALL_TILES
 
         def take_turn(turn):
-            if due(turn, 0):
-                regroup(turn)
-            if due(turn, LAG_QUANTISE):
-                quantise(turn - LAG_QUANTISE)
-            if due(turn, LAG_PROJECT_KEYS):
-                project_keys(turn - LAG_PROJECT_KEYS)
-            if due(turn, LAG_LEAVE_KEYS):
-                leave_keys(turn - LAG_LEAVE_KEYS)
-            if due(turn, LAG_PROJECT_VALUES):
-                project_values(turn - LAG_PROJECT_VALUES)
-            if due(turn, LAG_LEAVE_VALUES):
-                leave_values(turn - LAG_LEAVE_VALUES)
+            if due(turn, LAG_PROJECT):
+                project_keys(turn - LAG_PROJECT)
+                project_values(turn - LAG_PROJECT)
+            if due(turn, LAG_LEAVE):
+                leave_keys(turn - LAG_LEAVE)
+                leave_values(turn - LAG_LEAVE)
             if due(turn, LAG_POOL_VALUES):
                 pool_values(turn - LAG_POOL_VALUES)
             if due(turn, LAG_POOL_KEYS):
                 pool_keys(turn - LAG_POOL_KEYS)
+            if due(turn, LAG_QUANTISE):
+                quantise(turn - LAG_QUANTISE)
+            if due(turn, 0):
+                regroup(turn)
 
-        for turn in range(TILES):
-            take_turn(turn)
-        wv_codes, wv_scales = quantise_weight(wv_rows, "wv", val_banks, "vals")
-        for turn in range(TILES, ALL_TILES + LAG_POOL_KEYS):
+        take_turn(0)
+        fold_norm()
+        wk_codes, wk_scales = quantise_weight(wk_grouped, "wk")
+        take_turn(1)
+        take_turn(2)
+        wv_codes, wv_scales = quantise_weight(flip_weight(wv_rows, "wv", val_banks, "vals"), "wv")
+        for turn in range(3, LAST_TURN):
             take_turn(turn)
 
         value = keep.tile([P, CV], F32, name="value")

@@ -59,6 +59,8 @@ def tile_apnb_pa_kernel(tc, feats, Wk, bk, gk, betak, mk, vk, Wv, bv, out_0, out
         total = ctx.enter_context(tc.psum_pool(name="total", bufs=1))
         ctx.enter_context(tc.manual_schedule())
 
+        bv_row_bf = keep.tile([P, CV], BF16, name="bv_row_bf")
+        nc.gpsimd.memset(bv_row_bf[:], 0.0)
         position = keep.tile([P, ALL_TILES], I32, name="position")
         nc.gpsimd.iota(position[:], pattern=[[P, ALL_TILES]], base=0, channel_multiplier=1)
         count = keep.tile([P, 64], F32, name="count")
@@ -67,22 +69,25 @@ def tile_apnb_pa_kernel(tc, feats, Wk, bk, gk, betak, mk, vk, Wv, bv, out_0, out
         )
         ident = keep.tile([P, P], F32, name="ident")
         make_identity(nc, ident[:])
+        pool = keep.tile([P, ALL_TILES, P], F32, name="pool")
+        nc.gpsimd.memset(pool[:], 0.0)
+        nc.gpsimd.memset(pool[:, :, 0:8], 1.0)
         cell_size = keep.tile([P, P], F32, name="cell_size")
         nc.gpsimd.memset(cell_size[:, TOKENS:P], 1.0)
         for s in LEVELS:
             nc.gpsimd.memset(cell_size[:, FIRST[s] : FIRST[s] + s * s], float(N // (s * s)))
 
-        params_bf = keep.tile([P, CK], BF16, name="params_bf")
-        nc.vector.memset(params_bf[:], 0.0)
-        for row, values in enumerate((bv, bk, gk, betak, mk, vk)):
-            nc.scalar.dma_start(out=params_bf[row : row + 1, :], in_=values.rearrange("(o c) -> o c", o=1))
+        by_channel = keep.tile([P, 5, 16], BF16, name="by_channel")
+        for v, values in enumerate((bk, gk, betak, mk, vk)):
+            nc.scalar.dma_start(out=by_channel[:, v, 0:HALVES], in_=values.rearrange("(p m) -> p m", m=HALVES))
+        nc.scalar.dma_start(out=bv_row_bf[0:1, :], in_=bv.rearrange("(o c) -> o c", o=1))
 
-        def load_weight(w, name):
+        def load_weight(rows_by_partition, name):
             rows = keep.tile([P, HALVES, C], BF16, name=name)
-            nc.sync.dma_start(out=rows[:], in_=w.rearrange("(r p) k -> p r k", p=P))
+            nc.sync.dma_start(out=rows[:], in_=rows_by_partition)
             return rows
 
-        wk_rows = load_weight(Wk, "wk_rows")
+        wk_rows = load_weight(Wk.rearrange("(p r) k -> p r k", r=HALVES), "wk_rows")
 
         x_rows = feats.rearrange("b (s q e) h w -> e q (b s) (h w)", s=2 * PASSES, e=2)
         raw = [keep.tile([P, PASSES, PACK, CHUNK], BF16, name="raw%d" % c) for c in range(CHUNKS)]
@@ -93,7 +98,7 @@ def tile_apnb_pa_kernel(tc, feats, Wk, bk, gk, betak, mk, vk, Wv, bv, out_0, out
                 nc.sync.dma_start(out=split[:, :, e, :], in_=x_rows[e][:, :, c * CHUNK : (c + 1) * CHUNK])
 
         load_chunk(0)
-        wv_rows = load_weight(Wv, "wv_rows")
+        wv_rows = load_weight(Wv.rearrange("(r p) k -> p r k", p=P), "wv_rows")
         load_chunk(1)
         load_chunk(2)
 
@@ -126,9 +131,6 @@ def tile_apnb_pa_kernel(tc, feats, Wk, bk, gk, betak, mk, vk, Wv, bv, out_0, out
         nc.vector.tensor_scalar(out=shifted[:], in0=place[:], scalar1=1, scalar2=None, op0=ALU.logical_shift_right)
         third(band_cell[:, 2], shifted[:], 0)
         cell = keep.tile([P, 3, ALL_TILES], F32, name="cell")
-        pool = keep.tile([P, ALL_TILES, P], F32, name="pool")
-        nc.vector.memset(pool[:, :, 0:1], 1.0)
-        nc.vector.memset(pool[:, :, TOKENS:P], 0.0)
         for l, s in enumerate(LEVELS[1:]):
             nc.vector.scalar_tensor_tensor(
                 out=cell[:, l, :],
@@ -147,19 +149,16 @@ def tile_apnb_pa_kernel(tc, feats, Wk, bk, gk, betak, mk, vk, Wv, bv, out_0, out
             )
         weight = keep.tile([P, P], F32, name="weight")
         nc.vector.reciprocal(out=weight[:], in_=cell_size[:])
-        nc.vector.tensor_tensor(
-            out=pool[:], in0=pool[:], in1=weight[:].unsqueeze(1).to_broadcast([P, ALL_TILES, P]), op=ALU.mult
-        )
 
-        def flip_weight(rows, name, psum, tag):
+        def flip_weight(rows, name, psum, tag, copies):
             w_grouped = keep.tile([P, PASSES, HALVES * P, PACK], BF16, name=name + "_grouped", align_bytes=64)
             w_pairs = w_grouped[:].bitcast(F32)
-            for r in range(HALVES):
+            for r, copy in enumerate(copies):
                 words = rows[:, r, :].bitcast(F32)
                 bank = psum.tile([P, BANK], F32, name=name + "_bank", tag=tag)
                 for s in range(BANK // P):
                     nc.tensor.transpose(bank[:, s * P : (s + 1) * P], words[:, s * P : (s + 1) * P], ident[:])
-                nc.scalar.copy(
+                copy(
                     out=w_pairs[:, :, r * P : (r + 1) * P, :],
                     in_=bank[:].rearrange("p (g u o) -> p g o u", g=PASSES, u=2),
                 )
@@ -175,39 +174,34 @@ def tile_apnb_pa_kernel(tc, feats, Wk, bk, gk, betak, mk, vk, Wv, bv, out_0, out
             )
             return codes, scales
 
-        params = keep.tile([P, CK], F32, name="params")
-        nc.vector.tensor_copy(out=params[:], in_=params_bf[:])
-        wk_grouped = flip_weight(wk_rows, "wk", key_banks, "keys")
+        wk_grouped = flip_weight(wk_rows, "wk", key_banks, "keys", (nc.vector.tensor_copy, nc.scalar.copy))
 
-        params_bank = val_banks.tile([P, BANK], F32, name="params_bank", tag="vals")
-        flipped_params = params_bank[:, 0 : HALVES * P].rearrange("p (m r) -> p m r", m=HALVES)
-        for m in range(HALVES):
-            nc.tensor.transpose(flipped_params[:, m, :], params[:, m * P : (m + 1) * P], ident[:])
-        by_channel = keep.tile([P, HALVES, 6], F32, name="by_channel")
+        bk_c, gk_c, betak_c, mk_c, vk_c = [by_channel[:, v, 0:HALVES] for v in range(5)]
         minus_half = keep.tile([P, HALVES], F32, name="minus_half")
         nc.gpsimd.memset(minus_half[:], -0.5)
         scale = keep.tile([P, HALVES], F32, name="scale")
         shift = keep.tile([P, HALVES], F32, name="shift")
+        nc.gpsimd.tensor_scalar_add(out=scale[:], in0=vk_c, scalar1=EPS)
+        nc.gpsimd.tensor_tensor(out=scale[:], in0=scale[:], in1=minus_half[:], op=ALU.pow)
+        nc.gpsimd.tensor_mul(out=scale[:], in0=scale[:], in1=gk_c)
+        nc.gpsimd.tensor_sub(out=shift[:], in0=bk_c, in1=mk_c)
+        nc.gpsimd.tensor_mul(out=shift[:], in0=shift[:], in1=scale[:])
+        nc.gpsimd.tensor_add(out=shift[:], in0=shift[:], in1=betak_c)
 
-        def fold_norm():
-            nc.scalar.copy(out=by_channel[:], in_=flipped_params[:, :, 0:6])
-            nc.gpsimd.tensor_scalar_add(out=scale[:], in0=by_channel[:, :, 5], scalar1=EPS)
-            nc.gpsimd.tensor_tensor(out=scale[:], in0=scale[:], in1=minus_half[:], op=ALU.pow)
-            nc.gpsimd.tensor_mul(out=scale[:], in0=scale[:], in1=by_channel[:, :, 2])
-            nc.gpsimd.tensor_sub(out=shift[:], in0=by_channel[:, :, 1], in1=by_channel[:, :, 4])
-            nc.gpsimd.tensor_mul(out=shift[:], in0=shift[:], in1=scale[:])
-            nc.gpsimd.tensor_add(out=shift[:], in0=shift[:], in1=by_channel[:, :, 3])
-
+        weight_bank = val_banks.tile([P, BANK], F32, name="weight_bank", tag="vals")
+        nc.tensor.transpose(weight_bank[:, 0:P], weight[:], ident[:])
+        token_weight = keep.tile([P, 1], F32, name="token_weight")
+        bv_row = keep.tile([P, CV], F32, name="bv_row")
+        nc.gpsimd.tensor_copy(out=bv_row[:], in_=bv_row_bf[:])
+        bias_pick = keep.tile([P, P], F32, name="bias_pick")
+        nc.gpsimd.tensor_scalar_mul(out=bias_pick[:], in0=cell_size[:], scalar1=ident[:, 0:1])
         value_sum = total.tile([P, BANK], F32, name="value_sum")
-        nc.tensor.matmul(
-            out=value_sum[:, 0:CV], lhsT=ident[:, 0:1].to_broadcast([P, P]), rhs=params[:], start=True, stop=False
-        )
 
         grouped = keep.tile([P, ALL_TILES, PASSES, P, PACK], BF16, name="grouped", align_bytes=64)
         x_codes = keep.tile([P, ALL_TILES, PASSES, P], U32, name="x_codes", align_bytes=64)
         x_scales = keep.tile([P, ALL_TILES, PASSES, P], U8, name="x_scales", align_bytes=64)
         kf = keep.tile([P, HALVES, N], F32, name="kf")
-        kf_out = out_0.rearrange("b (m p) h w -> p (b m) (h w)", p=P)
+        kf_out = out_0.rearrange("b (p m) h w -> p (b m) (h w)", m=HALVES)
         sums = keep.tile([P, HALVES, TOKENS], F32, name="sums")
         val_t = keep.tile([P, ALL_TILES, CV], F32, name="val_t")
         key_bank = {}
@@ -275,6 +269,8 @@ def tile_apnb_pa_kernel(tc, feats, Wk, bk, gk, betak, mk, vk, Wv, bv, out_0, out
                 nc.sync.dma_start(out=kf_out[:, :, cols], in_=kf[:, :, cols])
 
         def pool_values(i):
+            if i == 0:
+                nc.tensor.matmul(out=value_sum[:, 0:CV], lhsT=bias_pick[:], rhs=bv_row[:], start=True, stop=False)
             nc.tensor.matmul(
                 out=value_sum[:, 0:CV], lhsT=pool[:, i, :], rhs=val_t[:, i, :], start=False, stop=(i == ALL_TILES - 1)
             )
@@ -325,16 +321,16 @@ def tile_apnb_pa_kernel(tc, feats, Wk, bk, gk, betak, mk, vk, Wv, bv, out_0, out
                 regroup(turn)
 
         take_turn(0)
-        fold_norm()
+        nc.scalar.copy(out=token_weight[:], in_=weight_bank[:, 0:1])
         wk_codes, wk_scales = quantise_weight(wk_grouped, "wk")
         take_turn(1)
         take_turn(2)
-        wv_codes, wv_scales = quantise_weight(flip_weight(wv_rows, "wv", val_banks, "vals"), "wv")
+        wv_codes, wv_scales = quantise_weight(flip_weight(wv_rows, "wv", val_banks, "vals", (nc.scalar.copy, nc.scalar.copy)), "wv")
         for turn in range(3, LAST_TURN):
             take_turn(turn)
 
         value = keep.tile([P, CV], F32, name="value")
-        nc.scalar.copy(out=value[:], in_=value_sum[:, 0:CV])
+        nc.scalar.activation(out=value[:], in_=value_sum[:, 0:CV], func=ACT.Copy, scale=token_weight[:, 0:1])
         nc.sync.dma_start(out=out_2.rearrange("b t c -> (b t) c"), in_=value[0:TOKENS, :])
 
         nc.vector.tensor_reduce(out=sums[:, :, 0:1], in_=sums[:, :, FIRST[3] : FIRST[6]], axis=AXIS.X, op=ALU.add)
@@ -345,4 +341,4 @@ def tile_apnb_pa_kernel(tc, feats, Wk, bk, gk, betak, mk, vk, Wv, bv, out_0, out
             in1=weight[:, 0:TOKENS].unsqueeze(1).to_broadcast([P, HALVES, TOKENS]),
             op=ALU.mult,
         )
-        nc.sync.dma_start(out=out_1.rearrange("b (m p) t -> p (b m) t", p=P), in_=keyp[:])
+        nc.sync.dma_start(out=out_1.rearrange("b (p m) t -> p (b m) t", m=HALVES), in_=keyp[:])

@@ -69,13 +69,14 @@ def tile_apnb_pa_kernel(tc, feats, Wk, bk, gk, betak, mk, vk, Wv, bv, out_0, out
         )
         ident = keep.tile([P, P], F32, name="ident")
         make_identity(nc, ident[:])
-        pool = keep.tile([P, ALL_TILES, P], F32, name="pool")
-        nc.gpsimd.memset(pool[:], 0.0)
-        nc.gpsimd.memset(pool[:, :, 0:8], 1.0)
         cell_size = keep.tile([P, P], F32, name="cell_size")
         nc.gpsimd.memset(cell_size[:, TOKENS:P], 1.0)
         for s in LEVELS:
             nc.gpsimd.memset(cell_size[:, FIRST[s] : FIRST[s] + s * s], float(N // (s * s)))
+        bias_pick = keep.tile([P, P], F32, name="bias_pick")
+        nc.gpsimd.tensor_scalar(
+            out=bias_pick[:], in0=cell_size[:], scalar1=ident[:, 0:1], scalar2=0.0, op0=ALU.mult, op1=ALU.add
+        )
 
         by_channel = keep.tile([P, 5, 16], BF16, name="by_channel")
         for v, values in enumerate((bk, gk, betak, mk, vk)):
@@ -131,6 +132,9 @@ def tile_apnb_pa_kernel(tc, feats, Wk, bk, gk, betak, mk, vk, Wv, bv, out_0, out
         nc.vector.tensor_scalar(out=shifted[:], in0=place[:], scalar1=1, scalar2=None, op0=ALU.logical_shift_right)
         third(band_cell[:, 2], shifted[:], 0)
         cell = keep.tile([P, 3, ALL_TILES], F32, name="cell")
+        pool = keep.tile([P, ALL_TILES, P], F32, name="pool")
+        nc.vector.memset(pool[:, :, 0:1], 1.0)
+        nc.vector.memset(pool[:, :, TOKENS:P], 0.0)
         for l, s in enumerate(LEVELS[1:]):
             nc.vector.scalar_tensor_tensor(
                 out=cell[:, l, :],
@@ -192,9 +196,7 @@ def tile_apnb_pa_kernel(tc, feats, Wk, bk, gk, betak, mk, vk, Wv, bv, out_0, out
         nc.tensor.transpose(weight_bank[:, 0:P], weight[:], ident[:])
         token_weight = keep.tile([P, 1], F32, name="token_weight")
         bv_row = keep.tile([P, CV], F32, name="bv_row")
-        nc.gpsimd.tensor_copy(out=bv_row[:], in_=bv_row_bf[:])
-        bias_pick = keep.tile([P, P], F32, name="bias_pick")
-        nc.gpsimd.tensor_scalar_mul(out=bias_pick[:], in0=cell_size[:], scalar1=ident[:, 0:1])
+        nc.gpsimd.tensor_scalar(out=bv_row[:], in0=bv_row_bf[:], scalar1=1.0, scalar2=0.0, op0=ALU.mult, op1=ALU.add)
         value_sum = total.tile([P, BANK], F32, name="value_sum")
 
         grouped = keep.tile([P, ALL_TILES, PASSES, P, PACK], BF16, name="grouped", align_bytes=64)
@@ -202,6 +204,7 @@ def tile_apnb_pa_kernel(tc, feats, Wk, bk, gk, betak, mk, vk, Wv, bv, out_0, out
         x_scales = keep.tile([P, ALL_TILES, PASSES, P], U8, name="x_scales", align_bytes=64)
         kf = keep.tile([P, HALVES, N], F32, name="kf")
         kf_out = out_0.rearrange("b (p m) h w -> p (b m) (h w)", m=HALVES)
+        pairs = keep.tile([P, HALVES, N // 2], F32, name="pairs")
         sums = keep.tile([P, HALVES, TOKENS], F32, name="sums")
         val_t = keep.tile([P, ALL_TILES, CV], F32, name="val_t")
         key_bank = {}
@@ -288,14 +291,19 @@ def tile_apnb_pa_kernel(tc, feats, Wk, bk, gk, betak, mk, vk, Wv, bv, out_0, out
                     op=ALU.add,
                 )
                 return
+            if s == POOLED[0]:
+                two = kf[:, :, c * CHUNK : (c + 1) * CHUNK].rearrange("p m (q e) -> p m q e", e=2)
+                nc.vector.tensor_tensor(
+                    out=pairs[:, :, c * CHUNK // 2 : (c + 1) * CHUNK // 2], in0=two[:, :, :, 0], in1=two[:, :, :, 1], op=ALU.add
+                )
             rows = H // s
             first = c * CHUNK_ROWS // rows
             after = (c + 1) * CHUNK_ROWS // rows
             for m in range(HALVES):
                 nc.vector.tensor_reduce(
                     out=sums[:, m, FIRST[s] + first * s : FIRST[s] + after * s].rearrange("p (b c) -> p b c", c=s),
-                    in_=kf[:, m, first * rows * W : after * rows * W].rearrange(
-                        "p (b r c x) -> p b c r x", r=rows, c=s, x=W // s
+                    in_=pairs[:, m, first * rows * W // 2 : after * rows * W // 2].rearrange(
+                        "p (b r c x) -> p b c r x", r=rows, c=s, x=W // s // 2
                     ),
                     axis=AXIS.XY,
                     op=ALU.add,

from contextlib import ExitStack

import concourse.mybir as mybir
from concourse.masks import make_identity

F32 = mybir.dt.float32
BF16 = mybir.dt.bfloat16
I32 = mybir.dt.int32
U32 = mybir.dt.uint32
U8 = mybir.dt.uint8
FP8X4 = mybir.dt.float8_e4m3fn_x4
ALU = mybir.AluOpType
ACT = mybir.ActivationFunctionType
AXIS = mybir.AxisListType

P = 128
PACK = 4
K_PASS = P * PACK
BANK = 512

C = 1024
PASSES = C // K_PASS
CK = 256
CV = 256
HALVES = CK // P
H = 24
W = 48
N = H * W
EPS = 1e-5

CHUNK_ROWS = 8
CHUNK = CHUNK_ROWS * W
CHUNKS = N // CHUNK
TILES = CHUNK // P
ALL_TILES = CHUNKS * TILES

LEVELS = (1, 3, 6, 8)
FIRST = {1: 0, 3: 1, 6: 10, 8: 46}
TOKENS = 110

FLOPS = 2 * (CK + CV) * C * N


LAG_QUANTISE = 1
LAG_PROJECT = 3
LAG_LEAVE = 5
LAG_POOL_VALUES = 7
LAG_POOL_KEYS = 8
LAST_TURN = ALL_TILES + LAG_POOL_KEYS
POOLED = (8, 6, 3)


def tile_apnb_pa_kernel(tc, feats, Wk, bk, gk, betak, mk, vk, Wv, bv, out_0, out_1, out_2):
    nc = tc.nc
    with ExitStack() as ctx:
        keep = ctx.enter_context(tc.tile_pool(name="keep", bufs=1))
        key_banks = ctx.enter_context(tc.psum_pool(name="key_banks", bufs=2 * HALVES))
        val_banks = ctx.enter_context(tc.psum_pool(name="val_banks", bufs=3))
        total = ctx.enter_context(tc.psum_pool(name="total", bufs=1))
        ctx.enter_context(tc.manual_schedule())

        bv_row_bf = keep.tile([P, CV], BF16, name="bv_row_bf")
        nc.gpsimd.memset(bv_row_bf[:], 0.0)
        position = keep.tile([P, ALL_TILES], I32, name="position")
        nc.gpsimd.iota(position[:], pattern=[[P, ALL_TILES]], base=0, channel_multiplier=1)
        count = keep.tile([P, 64], F32, name="count")
        nc.gpsimd.iota(
            count[:], pattern=[[1, 64]], base=0, channel_multiplier=0, allow_small_or_imprecise_dtypes=True
        )
        ident = keep.tile([P, P], F32, name="ident")
        make_identity(nc, ident[:])
        cell_size = keep.tile([P, P], F32, name="cell_size")
        nc.gpsimd.memset(cell_size[:, TOKENS:P], 1.0)
        for s in LEVELS:
            nc.gpsimd.memset(cell_size[:, FIRST[s] : FIRST[s] + s * s], float(N // (s * s)))
        bias_pick = keep.tile([P, P], F32, name="bias_pick")
        nc.gpsimd.tensor_scalar(
            out=bias_pick[:], in0=cell_size[:], scalar1=ident[:, 0:1], scalar2=0.0, op0=ALU.mult, op1=ALU.add
        )

        by_channel = keep.tile([P, 5, 16], BF16, name="by_channel")
        for v, values in enumerate((bk, gk, betak, mk, vk)):
            nc.scalar.dma_start(out=by_channel[:, v, 0:HALVES], in_=values.rearrange("(p m) -> p m", m=HALVES))
        nc.scalar.dma_start(out=bv_row_bf[0:1, :], in_=bv.rearrange("(o c) -> o c", o=1))

        def load_weight(rows_by_partition, name):
            rows = keep.tile([P, HALVES, C], BF16, name=name)
            nc.sync.dma_start(out=rows[:], in_=rows_by_partition)
            return rows

        wk_rows = load_weight(Wk.rearrange("(p r) k -> p r k", r=HALVES), "wk_rows")

        x_rows = feats.rearrange("b (s q e) h w -> e q (b s) (h w)", s=2 * PASSES, e=2)
        raw = [keep.tile([P, PASSES, PACK, CHUNK], BF16, name="raw%d" % c) for c in range(CHUNKS)]

        def load_chunk(c):
            split = raw[c][:].rearrange("p g (u e) n -> p (g u) e n", e=2)
            for e in range(2):
                nc.sync.dma_start(out=split[:, :, e, :], in_=x_rows[e][:, :, c * CHUNK : (c + 1) * CHUNK])

        load_chunk(0)
        wv_rows = load_weight(Wv.rearrange("(r p) k -> p r k", p=P), "wv_rows")
        load_chunk(1)
        load_chunk(2)

        shifted = keep.tile([P, 2, ALL_TILES], I32, name="shifted")
        product = keep.tile([P, 2, ALL_TILES], I32, name="product")

        def third(out, in_, also_shift_left):
            like = product[:, 0 : in_.shape[1], :]
            nc.vector.tensor_scalar(out=like, in0=in_, scalar1=683.0, scalar2=None, op0=ALU.mult)
            nc.vector.tensor_scalar(
                out=out,
                in0=like,
                scalar1=11,
                scalar2=also_shift_left,
                op0=ALU.logical_shift_right,
                op1=ALU.logical_shift_left,
            )

        place = keep.tile([P, 2, ALL_TILES], I32, name="place")
        nc.vector.tensor_scalar(
            out=shifted[:, 0:1, :], in0=position[:].unsqueeze(1), scalar1=4, scalar2=None, op0=ALU.logical_shift_right
        )
        third(place[:, 0:1, :], shifted[:, 0:1, :], 1)
        nc.vector.scalar_tensor_tensor(
            out=place[:, 1, :], in0=place[:, 0, :], scalar=-24.0, in1=position[:], op0=ALU.mult, op1=ALU.add
        )
        band_cell = keep.tile([P, 3, 2, ALL_TILES], I32, name="band_cell")
        nc.vector.tensor_scalar(out=band_cell[:, 0], in0=place[:], scalar1=4, scalar2=None, op0=ALU.logical_shift_right)
        nc.vector.tensor_scalar(out=band_cell[:, 1], in0=place[:], scalar1=3, scalar2=None, op0=ALU.logical_shift_right)
        nc.vector.tensor_scalar(out=shifted[:], in0=place[:], scalar1=1, scalar2=None, op0=ALU.logical_shift_right)
        third(band_cell[:, 2], shifted[:], 0)
        cell = keep.tile([P, 3, ALL_TILES], F32, name="cell")
        pool = keep.tile([P, ALL_TILES, P], F32, name="pool")
        nc.vector.memset(pool[:, :, 0:1], 1.0)
        nc.vector.memset(pool[:, :, TOKENS:P], 0.0)
        for l, s in enumerate(LEVELS[1:]):
            nc.vector.scalar_tensor_tensor(
                out=cell[:, l, :],
                in0=band_cell[:, l, 0, :],
                scalar=float(s),
                in1=band_cell[:, l, 1, :],
                op0=ALU.mult,
                op1=ALU.add,
            )
            shape = [P, ALL_TILES, s * s]
            nc.vector.tensor_tensor(
                out=pool[:, :, FIRST[s] : FIRST[s] + s * s],
                in0=count[:, 0 : s * s].unsqueeze(1).to_broadcast(shape),
                in1=cell[:, l, :].unsqueeze(2).to_broadcast(shape),
                op=ALU.is_equal,
            )
        weight = keep.tile([P, P], F32, name="weight")
        nc.vector.reciprocal(out=weight[:], in_=cell_size[:])

        def flip_weight(rows, name, psum, tag, copies):
            w_grouped = keep.tile([P, PASSES, HALVES * P, PACK], BF16, name=name + "_grouped", align_bytes=64)
            w_pairs = w_grouped[:].bitcast(F32)
            for r, copy in enumerate(copies):
                words = rows[:, r, :].bitcast(F32)
                bank = psum.tile([P, BANK], F32, name=name + "_bank", tag=tag)
                for s in range(BANK // P):
                    nc.tensor.transpose(bank[:, s * P : (s + 1) * P], words[:, s * P : (s + 1) * P], ident[:])
                copy(
                    out=w_pairs[:, :, r * P : (r + 1) * P, :],
                    in_=bank[:].rearrange("p (g u o) -> p g o u", g=PASSES, u=2),
                )
            return w_grouped

        def quantise_weight(w_grouped, name):
            codes = keep.tile([P, PASSES, HALVES * P], U32, name=name + "_codes", align_bytes=64)
            scales = keep.tile([P, PASSES, HALVES * P], U8, name=name + "_scales", align_bytes=64)
            nc.vector.quantize_mx(
                out=codes[:].rearrange("p g o -> p (g o)").bitcast(FP8X4),
                scales=scales[:].rearrange("p g o -> p (g o)"),
                in_=w_grouped[:].rearrange("p g o t -> p (g o t)"),
            )
            return codes, scales

        wk_grouped = flip_weight(wk_rows, "wk", key_banks, "keys", (nc.vector.tensor_copy, nc.scalar.copy))

        bk_c, gk_c, betak_c, mk_c, vk_c = [by_channel[:, v, 0:HALVES] for v in range(5)]
        minus_half = keep.tile([P, HALVES], F32, name="minus_half")
        nc.gpsimd.memset(minus_half[:], -0.5)
        scale = keep.tile([P, HALVES], F32, name="scale")
        shift = keep.tile([P, HALVES], F32, name="shift")
        nc.gpsimd.tensor_scalar_add(out=scale[:], in0=vk_c, scalar1=EPS)
        nc.gpsimd.tensor_tensor(out=scale[:], in0=scale[:], in1=minus_half[:], op=ALU.pow)
        nc.gpsimd.tensor_mul(out=scale[:], in0=scale[:], in1=gk_c)
        nc.gpsimd.tensor_sub(out=shift[:], in0=bk_c, in1=mk_c)
        nc.gpsimd.tensor_mul(out=shift[:], in0=shift[:], in1=scale[:])
        nc.gpsimd.tensor_add(out=shift[:], in0=shift[:], in1=betak_c)

        weight_bank = val_banks.tile([P, BANK], F32, name="weight_bank", tag="vals")
        nc.tensor.transpose(weight_bank[:, 0:P], weight[:], ident[:])
        token_weight = keep.tile([P, 1], F32, name="token_weight")
        bv_row = keep.tile([P, CV], F32, name="bv_row")
        nc.gpsimd.tensor_scalar(out=bv_row[:], in0=bv_row_bf[:], scalar1=1.0, scalar2=0.0, op0=ALU.mult, op1=ALU.add)
        value_sum = total.tile([P, BANK], F32, name="value_sum")

        grouped = keep.tile([P, ALL_TILES, PASSES, P, PACK], BF16, name="grouped", align_bytes=64)
        x_codes = keep.tile([P, ALL_TILES, PASSES, P], U32, name="x_codes", align_bytes=64)
        x_scales = keep.tile([P, ALL_TILES, PASSES, P], U8, name="x_scales", align_bytes=64)
        kf = keep.tile([P, HALVES, N], F32, name="kf")
        kf_out = out_0.rearrange("b (p m) h w -> p (b m) (h w)", m=HALVES)
        pairs = keep.tile([P, HALVES, N // 2], F32, name="pairs")
        sums = keep.tile([P, HALVES, TOKENS], F32, name="sums")
        val_t = keep.tile([P, ALL_TILES, CV], F32, name="val_t")
        key_bank = {}
        val_bank = {}

        def regroup(i):
            c, j = divmod(i, TILES)
            for g, copy in enumerate((nc.vector.tensor_copy, nc.scalar.copy)):
                copy(
                    out=grouped[:, i, g].rearrange("p (n r) t -> p n t r", r=4),
                    in_=raw[c][:, g, :, j * P : (j + 1) * P].rearrange("p t (n r) -> p n t r", r=4),
                )

        def quantise(i):
            nc.vector.quantize_mx(
                out=x_codes[:, i].rearrange("p g n -> p (g n)").bitcast(FP8X4),
                scales=x_scales[:, i].rearrange("p g n -> p (g n)"),
                in_=grouped[:, i].rearrange("p g n t -> p (g n t)"),
            )

        def project_keys(i):
            c, j = divmod(i, TILES)
            for m in range(HALVES):
                if j == 0:
                    key_bank[c, m] = key_banks.tile([P, BANK], F32, name="key_bank", tag="keys")
                for g in range(PASSES):
                    nc.tensor.matmul_mx(
                        out=key_bank[c, m][:, j * P : (j + 1) * P],
                        lhsT=wk_codes[:, g, m * P : (m + 1) * P].bitcast(FP8X4),
                        lhsT_scale=wk_scales[:, g, m * P : (m + 1) * P],
                        rhs=x_codes[:, i, g, :].bitcast(FP8X4),
                        rhs_scale=x_scales[:, i, g, :],
                        start=(g == 0),
                        stop=(g == PASSES - 1),
                    )

        def project_values(i):
            val_bank[i] = val_banks.tile([P, BANK], F32, name="val_bank", tag="vals")
            for g in range(PASSES):
                nc.tensor.matmul_mx(
                    out=val_bank[i][:, 0:CV],
                    lhsT=x_codes[:, i, g, :].bitcast(FP8X4),
                    lhsT_scale=x_scales[:, i, g, :],
                    rhs=wv_codes[:, g, :].bitcast(FP8X4),
                    rhs_scale=wv_scales[:, g, :],
                    start=(g == 0),
                    stop=(g == PASSES - 1),
                )

        def leave_values(i):
            nc.scalar.copy(out=val_t[:, i, :], in_=val_bank[i][:, 0:CV])

        def leave_keys(i):
            c, j = divmod(i, TILES)
            if j == TILES - 1:
                cols = slice(c * CHUNK, (c + 1) * CHUNK)
                for m in range(HALVES):
                    nc.scalar.activation(
                        out=kf[:, m, cols],
                        in_=key_bank[c, m][:, 0:CHUNK],
                        func=ACT.Relu,
                        bias=shift[:, m : m + 1],
                        scale=scale[:, m : m + 1],
                    )
                nc.sync.dma_start(out=kf_out[:, :, cols], in_=kf[:, :, cols])

        def pool_values(i):
            if i == 0:
                nc.tensor.matmul(out=value_sum[:, 0:CV], lhsT=bias_pick[:], rhs=bv_row[:], start=True, stop=False)
            nc.tensor.matmul(
                out=value_sum[:, 0:CV], lhsT=pool[:, i, :], rhs=val_t[:, i, :], start=False, stop=(i == ALL_TILES - 1)
            )

        def pool_keys(i):
            c, j = divmod(i, TILES)
            s = POOLED[j]
            if s == 3:
                nc.vector.tensor_reduce(
                    out=sums[:, :, FIRST[3] + 3 * c : FIRST[3] + 3 * (c + 1)],
                    in_=sums[:, :, FIRST[6] + 12 * c : FIRST[6] + 12 * (c + 1)].rearrange(
                        "p m (b c x) -> p m c b x", b=2, x=2
                    ),
                    axis=AXIS.XY,
                    op=ALU.add,
                )
                return
            if s == POOLED[0]:
                two = kf[:, :, c * CHUNK : (c + 1) * CHUNK].rearrange("p m (q e) -> p m q e", e=2)
                nc.vector.tensor_tensor(
                    out=pairs[:, :, c * CHUNK // 2 : (c + 1) * CHUNK // 2], in0=two[:, :, :, 0], in1=two[:, :, :, 1], op=ALU.add
                )
            rows = H // s
            first = c * CHUNK_ROWS // rows
            after = (c + 1) * CHUNK_ROWS // rows
            for m in range(HALVES):
                nc.vector.tensor_reduce(
                    out=sums[:, m, FIRST[s] + first * s : FIRST[s] + after * s].rearrange("p (b c) -> p b c", c=s),
                    in_=pairs[:, m, first * rows * W // 2 : after * rows * W // 2].rearrange(
                        "p (b r c x) -> p b c r x", r=rows, c=s, x=W // s // 2
                    ),
                    axis=AXIS.XY,
                    op=ALU.add,
                )

        def due(turn, lag):
            return 0 <= turn - lag < ALL_TILES

        def take_turn(turn):
            if due(turn, LAG_PROJECT):
                project_keys(turn - LAG_PROJECT)
                project_values(turn - LAG_PROJECT)
            if due(turn, LAG_LEAVE):
                leave_keys(turn - LAG_LEAVE)
                leave_values(turn - LAG_LEAVE)
            if due(turn, LAG_POOL_VALUES):
                pool_values(turn - LAG_POOL_VALUES)
            if due(turn, LAG_POOL_KEYS):
                pool_keys(turn - LAG_POOL_KEYS)
            if due(turn, LAG_QUANTISE):
                quantise(turn - LAG_QUANTISE)
            if due(turn, 0):
                regroup(turn)

        take_turn(0)
        nc.scalar.copy(out=token_weight[:], in_=weight_bank[:, 0:1])
        wk_codes, wk_scales = quantise_weight(wk_grouped, "wk")
        take_turn(1)
        take_turn(2)
        wv_codes, wv_scales = quantise_weight(flip_weight(wv_rows, "wv", val_banks, "vals", (nc.scalar.copy, nc.scalar.copy)), "wv")
        for turn in range(3, LAST_TURN):
            take_turn(turn)

        value = keep.tile([P, CV], F32, name="value")
        nc.scalar.activation(out=value[:], in_=value_sum[:, 0:CV], func=ACT.Copy, scale=token_weight[:, 0:1])
        nc.sync.dma_start(out=out_2.rearrange("b t c -> (b t) c"), in_=value[0:TOKENS, :])

        nc.vector.tensor_reduce(out=sums[:, :, 0:1], in_=sums[:, :, FIRST[3] : FIRST[6]], axis=AXIS.X, op=ALU.add)
        keyp = keep.tile([P, HALVES, TOKENS], F32, name="keyp")
        nc.vector.tensor_tensor(
            out=keyp[:],
            in0=sums[:],
            in1=weight[:, 0:TOKENS].unsqueeze(1).to_broadcast([P, HALVES, TOKENS]),
            op=ALU.mult,
        )
        nc.sync.dma_start(out=out_1.rearrange("b (p m) t -> p (b m) t", m=HALVES), in_=keyp[:])
